import numpy as np
import ml_dtypes


def mxq(x, axis, fmt="e4m3"):
    dtype, down = {"e4m3": (ml_dtypes.float8_e4m3fn, 7), "e5m2": (ml_dtypes.float8_e5m2, 14)}[fmt]
    v = np.moveaxis(np.asarray(x, np.float32).astype(ml_dtypes.bfloat16).astype(np.float64), axis, -1)
    blocks = v.reshape(v.shape[:-1] + (-1, 32))
    amax = np.abs(blocks).max(-1, keepdims=True)
    byte = np.maximum(np.where(amax > 0, np.frexp(amax)[1] - 1 + 127, 0) - down, 1)
    scale = np.exp2(byte - 127.0)
    codes = (blocks / scale).astype(np.float32).astype(dtype).astype(np.float64)
    return np.moveaxis((codes * scale).reshape(v.shape), -1, axis)


WIDE = False


def mx_kscale(k):
    if not WIDE:
        return np.ones(k)
    levels = np.array([10, -10, 5, -5, 0])
    a = np.random.permutation(np.resize(levels, k // 512 * 4)).reshape(k // 512, 4)
    idx = np.arange(k)
    return np.exp2(a[idx // 512, idx % 128 // 32])


BF16 = ml_dtypes.bfloat16


def bf(x):
    return np.asarray(x, np.float32).astype(BF16)


def f64(x):
    return np.asarray(x).astype(np.float64)


BS, NB, BD, H = 512, 4, 512, 1024
D = NB * BD
G = BS * NB // BD
ZMAX, NTERMS = 6.0, 120


def erf(z):
    a = np.minimum(np.abs(z), ZMAX)
    q = a * a
    term = a.copy()
    tot = a.copy()
    for n in range(1, NTERMS):
        term = term * q / (n + 0.5)
        tot = tot + term
    return np.sign(z) * np.minimum(tot * np.exp(-q) / (0.5 * np.sqrt(np.pi)), 1.0)


def gelu(v):
    return 0.5 * v * (1.0 + erf(v * np.sqrt(0.5)))


def setup_inputs():
    s = mx_kscale(BD)
    y = np.random.standard_normal((G, BD, BD)) * s[None, :, None]
    return {"y0": bf(y.reshape(BS, D)),
            "W1": bf(np.random.standard_normal((NB, BD, H)) / np.sqrt(BD) / s[None, :, None]),
            "b1": bf(np.random.standard_normal((NB, 1, H)) * 0.2),
            "W2": bf(np.random.standard_normal((NB, H, BD)) * 1.5 / np.sqrt(H)),
            "b2": bf(np.random.standard_normal((NB, 1, BD)) * 0.2)}


def reference(y0, W1, b1, W2, b2):
    z = f64(y0).reshape(-1, BD, BD).transpose(0, 2, 1).reshape(BS, -1)
    zb = z.reshape(BS, NB, BD).transpose(1, 0, 2)
    h = gelu((mxq(zb, 2, "e4m3") @ mxq(f64(W1), 1, "e4m3")) + f64(b1))
    o = (mxq(h, 2, "e4m3") @ mxq(f64(W2), 1, "e4m3")) + f64(b2)
    o = o.transpose(1, 0, 2).reshape(BS, -1)
    return o.reshape(-1, BD, BD).transpose(0, 2, 1).reshape(BS, -1)

@@ -1,0 +1,217 @@
+from contextlib import ExitStack
+
+import concourse.mybir as mybir
+from concourse.masks import make_identity
+
+BF16 = mybir.dt.bfloat16
+F32 = mybir.dt.float32
+U32 = mybir.dt.uint32
+U8 = mybir.dt.uint8
+FP8X4 = mybir.dt.float8_e4m3fn_x4
+GELU = mybir.ActivationFunctionType.Gelu
+ADD = mybir.AluOpType.add
+
+P = 128
+PACK = 4
+K_PASS = P * PACK
+
+BS, NB, BD, H = 512, 4, 512, 1024
+G = BS * NB // BD
+H_CHUNKS = H // P
+H_PASSES = H // K_PASS
+I_CHUNKS = BD // P
+HALF_H = H // 2
+HALF_I = BD // 2
+RUN = 4
+
+FLOPS = 2 * BS * NB * (BD * H + H * BD)
+
+
+def regroup(copy, grouped, planes):
+    copy(
+        out=grouped.rearrange("p (c i) t -> p c t i", i=RUN),
+        in_=planes.rearrange("p t (c i) -> p c t i", i=RUN),
+    )
+
+
+def tile_blockmlp_mixerblock_pa_kernel(tc, y0, W1, b1, W2, b2, out):
+    nc = tc.nc
+    out_rows = out.rearrange("a b -> (a b)").rearrange("(g i c) -> g i c", g=G, i=BD)
+
+    def quantise(grouped_flat, codes, scales):
+        nc.vector.quantize_mx(out=codes.bitcast(FP8X4), scales=scales, in_=grouped_flat)
+
+    with ExitStack() as ctx:
+        keep = ctx.enter_context(tc.tile_pool(name="keep", bufs=1))
+        by_vector = ctx.enter_context(tc.tile_pool(name="by_vector", bufs=4))
+        by_scalar = ctx.enter_context(tc.tile_pool(name="by_scalar", bufs=4))
+        hidden = ctx.enter_context(tc.tile_pool(name="hidden", bufs=3))
+        results = ctx.enter_context(tc.tile_pool(name="results", bufs=6))
+        psum_bias = ctx.enter_context(tc.psum_pool(name="psum_bias", bufs=1))
+        psum_h = ctx.enter_context(tc.psum_pool(name="psum_h", bufs=4))
+        psum_o = ctx.enter_context(tc.psum_pool(name="psum_o", bufs=3))
+
+        warm = keep.tile([P, 2], F32)
+        nc.vector.memset(warm[:], 0.0)
+        nc.scalar.activation(out=warm[:, 1:2], in_=warm[:, 0:1], func=GELU)
+
+        bias_rows = keep.tile([P, P], BF16)
+        nc.vector.memset(bias_rows[:], 0.0)
+        b1_rows = NB * H_CHUNKS
+        b2_rows = NB * I_CHUNKS
+        nc.scalar.dma_start(out=bias_rows[0:b1_rows, :], in_=b1.rearrange("n o (c p) -> (n o c) p", p=P))
+        nc.scalar.dma_start(
+            out=bias_rows[b1_rows : b1_rows + b2_rows, :], in_=b2.rearrange("n o (c p) -> (n o c) p", p=P)
+        )
+
+        y_raw = [keep.tile([P, PACK * BD], BF16, name="y_raw%d" % g) for g in range(G)]
+        w1_raw = [keep.tile([P, PACK, H], BF16, name="w1_raw%d" % n) for n in range(NB)]
+        w2_raw = [keep.tile([P, H_PASSES, PACK, BD], BF16, name="w2_raw%d" % n) for n in range(NB)]
+
+        def load_w1(n):
+            nc.sync.dma_start(out=w1_raw[n][:], in_=W1[n].rearrange("(p t) j -> p t j", t=PACK))
+
+        def load_w2(n):
+            nc.sync.dma_start(
+                out=w2_raw[n][:], in_=W2[n].rearrange("(s t p) i -> p s t i", s=H_PASSES, t=PACK)
+            )
+
+        for g in range(G):
+            nc.sync.dma_start(out=y_raw[g][:], in_=y0[g * P : (g + 1) * P, :])
+        load_w1(0)
+        for n in range(NB):
+            if n + 1 < NB:
+                load_w1(n + 1)
+            load_w2(n)
+
+        ident = keep.tile([P, P], BF16)
+        make_identity(nc, ident[:])
+        bias_t = psum_bias.tile([P, P], BF16)
+        nc.tensor.transpose(bias_t[:], bias_rows[:], ident[:])
+        b1_col = keep.tile([P, b1_rows], F32)
+        nc.vector.tensor_copy(out=b1_col[:], in_=bias_t[:, 0:b1_rows])
+        b2_col = keep.tile([P, I_CHUNKS, NB], F32)
+        nc.vector.tensor_copy(
+            out=b2_col[:], in_=bias_t[:, b1_rows : b1_rows + b2_rows].rearrange("p (n c) -> p c n", n=NB)
+        )
+
+        z_codes = keep.tile([P, NB, BS], U32, align_bytes=64)
+        z_scales = keep.tile([P, NB, BS], U8, align_bytes=64)
+        for g in range(G):
+            if g % 2 == 0:
+                z_grouped = by_vector.tile([P, NB, P, PACK], BF16, align_bytes=64, tag="grouped")
+                copy = nc.vector.tensor_copy
+            else:
+                z_grouped = by_scalar.tile([P, NB, P, PACK], BF16, align_bytes=64, tag="grouped")
+                copy = nc.scalar.copy
+            copy(
+                out=z_grouped[:].rearrange("p n r t -> p r t n"),
+                in_=y_raw[g][:].rearrange("p (t r n) -> p r t n", t=PACK, n=NB),
+            )
+            b_cols = slice(g * P, (g + 1) * P)
+            for n in range(NB):
+                quantise(
+                    z_grouped[:, n, :, :].rearrange("p r t -> p (r t)"), z_codes[:, n, b_cols], z_scales[:, n, b_cols]
+                )
+
+        w1_codes = [keep.tile([P, H], U32, align_bytes=64, name="w1_codes%d" % n) for n in range(NB)]
+        w1_scales = [keep.tile([P, H], U8, align_bytes=64, name="w1_scales%d" % n) for n in range(NB)]
+
+        def prepare_w1(n):
+            for half, (pool, copy) in enumerate(
+                ((by_vector, nc.vector.tensor_copy), (by_scalar, nc.scalar.copy))
+            ):
+                j_cols = slice(half * HALF_H, (half + 1) * HALF_H)
+                w_grouped = pool.tile([P, HALF_H, PACK], BF16, align_bytes=64, tag="grouped")
+                regroup(copy, w_grouped[:], w1_raw[n][:, :, j_cols])
+                quantise(
+                    w_grouped[:].rearrange("p c t -> p (c t)"), w1_codes[n][:, j_cols], w1_scales[n][:, j_cols]
+                )
+
+        w2_codes = [
+            [keep.tile([P, H_PASSES, HALF_I], U32, align_bytes=64, name="w2_codes%d_%d" % (half, n)) for n in range(NB)]
+            for half in range(2)
+        ]
+        w2_scales = [
+            [keep.tile([P, H_PASSES, HALF_I], U8, align_bytes=64, name="w2_scales%d_%d" % (half, n)) for n in range(NB)]
+            for half in range(2)
+        ]
+
+        def prepare_w2(n, half, pool, copy):
+            i_cols = slice(half * HALF_I, (half + 1) * HALF_I)
+            w_grouped = pool.tile([P, H_PASSES, HALF_I, PACK], BF16, align_bytes=64, tag="grouped")
+            for s in range(H_PASSES):
+                regroup(copy, w_grouped[:, s, :, :], w2_raw[n][:, s, :, i_cols])
+            quantise(
+                w_grouped[:].rearrange("p s c t -> p (s c t)"),
+                w2_codes[half][n][:].rearrange("p s c -> p (s c)"),
+                w2_scales[half][n][:].rearrange("p s c -> p (s c)"),
+            )
+
+        h_codes = [keep.tile([P, H_PASSES, BS], U32, align_bytes=64, name="h_codes%d" % n) for n in range(NB)]
+        h_scales = [keep.tile([P, H_PASSES, BS], U8, align_bytes=64, name="h_scales%d" % n) for n in range(NB)]
+
+        def first_layer(n):
+            for s in range(H_PASSES):
+                h_planes = hidden.tile([P, PACK, BS], BF16)
+                for t in range(PACK):
+                    chunk = s * PACK + t
+                    j_cols = slice(chunk * P, (chunk + 1) * P)
+                    h_acc = psum_h.tile([P, BS], F32)
+                    nc.tensor.matmul_mx(
+                        out=h_acc[:],
+                        lhsT=w1_codes[n][:, j_cols].bitcast(FP8X4),
+                        lhsT_scale=w1_scales[n][:, j_cols],
+                        rhs=z_codes[:, n, :].bitcast(FP8X4),
+                        rhs_scale=z_scales[:, n, :],
+                        start=True,
+                        stop=True,
+                    )
+                    bias_at = n * H_CHUNKS + chunk
+                    nc.scalar.activation(
+                        out=h_planes[:, t, :], in_=h_acc[:], func=GELU, bias=b1_col[:, bias_at : bias_at + 1], scale=1.0
+                    )
+                h_grouped = by_vector.tile([P, BS, PACK], BF16, align_bytes=64, tag="grouped")
+                regroup(nc.vector.tensor_copy, h_grouped[:], h_planes[:])
+                quantise(h_grouped[:].rearrange("p c t -> p (c t)"), h_codes[n][:, s, :], h_scales[n][:, s, :])
+
+        def second_layer(chunk, g):
+            half, within = divmod(chunk, I_CHUNKS // 2)
+            i_cols = slice(within * P, (within + 1) * P)
+            b_cols = slice(g * P, (g + 1) * P)
+            o_acc = psum_o.tile([P, NB, P], F32)
+            for n in range(NB):
+                for s in range(H_PASSES):
+                    nc.tensor.matmul_mx(
+                        out=o_acc[:, n, :],
+                        lhsT=w2_codes[half][n][:, s, i_cols].bitcast(FP8X4),
+                        lhsT_scale=w2_scales[half][n][:, s, i_cols],
+                        rhs=h_codes[n][:, s, b_cols].bitcast(FP8X4),
+                        rhs_scale=h_scales[n][:, s, b_cols],
+                        start=(s == 0),
+                        stop=(s == H_PASSES - 1),
+                    )
+            o_rows = results.tile([P, P, NB], F32)
+            nc.vector.tensor_tensor(
+                out=o_rows[:],
+                in0=o_acc[:].rearrange("p n r -> p r n"),
+                in1=b2_col[:, chunk, :].unsqueeze(1).to_broadcast([P, P, NB]),
+                op=ADD,
+            )
+            nc.sync.dma_start(
+                out=out_rows[g, chunk * P : (chunk + 1) * P, :], in_=o_rows[:].rearrange("p r n -> p (r n)")
+            )
+
+        prepare_w1(0)
+        for n in range(NB):
+            if n + 1 < NB:
+                prepare_w1(n + 1)
+            first_layer(n)
+            prepare_w2(n, 0, by_vector, nc.vector.tensor_copy)
+        for half in range(2):
+            if half == 1:
+                for n in range(NB):
+                    prepare_w2(n, 1, by_scalar, nc.scalar.copy)
+            for within in range(I_CHUNKS // 2):
+                for g in range(G):
+                    second_layer(half * (I_CHUNKS // 2) + within, g)

@@ -22,6 +22,9 @@ H_PASSES = H // K_PASS
 I_CHUNKS = BD // P
 HALF_H = H // 2
 HALF_I = BD // 2
+B_HALVES = 2
+HB = BS // B_HALVES
+G_HALF = G // B_HALVES
 RUN = 4
 
 FLOPS = 2 * BS * NB * (BD * H + H * BD)
@@ -45,11 +48,12 @@ def tile_blockmlp_mixerblock_pa_kernel(tc, y0, W1, b1, W2, b2, out):
         keep = ctx.enter_context(tc.tile_pool(name="keep", bufs=1))
         by_vector = ctx.enter_context(tc.tile_pool(name="by_vector", bufs=4))
         by_scalar = ctx.enter_context(tc.tile_pool(name="by_scalar", bufs=4))
-        hidden = ctx.enter_context(tc.tile_pool(name="hidden", bufs=3))
+        hidden = ctx.enter_context(tc.tile_pool(name="hidden", bufs=4))
         results = ctx.enter_context(tc.tile_pool(name="results", bufs=6))
         psum_bias = ctx.enter_context(tc.psum_pool(name="psum_bias", bufs=1))
         psum_h = ctx.enter_context(tc.psum_pool(name="psum_h", bufs=4))
         psum_o = ctx.enter_context(tc.psum_pool(name="psum_o", bufs=3))
+        ctx.enter_context(tc.manual_schedule())
 
         warm = keep.tile([P, 2], F32)
         nc.vector.memset(warm[:], 0.0)
@@ -59,135 +63,212 @@ def tile_blockmlp_mixerblock_pa_kernel(tc, y0, W1, b1, W2, b2, out):
         nc.vector.memset(bias_rows[:], 0.0)
         b1_rows = NB * H_CHUNKS
         b2_rows = NB * I_CHUNKS
-        nc.scalar.dma_start(out=bias_rows[0:b1_rows, :], in_=b1.rearrange("n o (c p) -> (n o c) p", p=P))
-        nc.scalar.dma_start(
-            out=bias_rows[b1_rows : b1_rows + b2_rows, :], in_=b2.rearrange("n o (c p) -> (n o c) p", p=P)
-        )
 
         y_raw = [keep.tile([P, PACK * BD], BF16, name="y_raw%d" % g) for g in range(G)]
         w1_raw = [keep.tile([P, PACK, H], BF16, name="w1_raw%d" % n) for n in range(NB)]
         w2_raw = [keep.tile([P, H_PASSES, PACK, BD], BF16, name="w2_raw%d" % n) for n in range(NB)]
 
-        def load_w1(n):
-            nc.sync.dma_start(out=w1_raw[n][:], in_=W1[n].rearrange("(p t) j -> p t j", t=PACK))
+        def load_y(g):
+            nc.sync.dma_start(out=y_raw[g][:], in_=y0[g * P : (g + 1) * P, :])
+
+        def load_w1(n, half):
+            j_cols = slice(half * HALF_H, (half + 1) * HALF_H)
+            nc.sync.dma_start(
+                out=w1_raw[n][:, :, j_cols], in_=W1[n][:, j_cols].rearrange("(p t) j -> p t j", t=PACK)
+            )
 
         def load_w2(n):
             nc.sync.dma_start(
                 out=w2_raw[n][:], in_=W2[n].rearrange("(s t p) i -> p s t i", s=H_PASSES, t=PACK)
             )
 
-        for g in range(G):
-            nc.sync.dma_start(out=y_raw[g][:], in_=y0[g * P : (g + 1) * P, :])
-        load_w1(0)
+        load_y(0)
+        load_y(1)
+        nc.sync.dma_start(out=bias_rows[0:b1_rows, :], in_=b1.rearrange("n o (c p) -> (n o c) p", p=P))
+        nc.sync.dma_start(
+            out=bias_rows[b1_rows : b1_rows + b2_rows, :], in_=b2.rearrange("n o (c p) -> (n o c) p", p=P)
+        )
         for n in range(NB):
-            if n + 1 < NB:
-                load_w1(n + 1)
-            load_w2(n)
+            for half in range(2):
+                load_w1(n, half)
+        load_w2(0)
+        load_w2(1)
+        load_y(2)
+        load_y(3)
+        load_w2(2)
+        load_w2(3)
 
         ident = keep.tile([P, P], BF16)
         make_identity(nc, ident[:])
         bias_t = psum_bias.tile([P, P], BF16)
-        nc.tensor.transpose(bias_t[:], bias_rows[:], ident[:])
         b1_col = keep.tile([P, b1_rows], F32)
-        nc.vector.tensor_copy(out=b1_col[:], in_=bias_t[:, 0:b1_rows])
         b2_col = keep.tile([P, I_CHUNKS, NB], F32)
-        nc.vector.tensor_copy(
-            out=b2_col[:], in_=bias_t[:, b1_rows : b1_rows + b2_rows].rearrange("p (n c) -> p c n", n=NB)
-        )
 
-        z_codes = keep.tile([P, NB, BS], U32, align_bytes=64)
-        z_scales = keep.tile([P, NB, BS], U8, align_bytes=64)
-        for g in range(G):
-            if g % 2 == 0:
-                z_grouped = by_vector.tile([P, NB, P, PACK], BF16, align_bytes=64, tag="grouped")
-                copy = nc.vector.tensor_copy
-            else:
-                z_grouped = by_scalar.tile([P, NB, P, PACK], BF16, align_bytes=64, tag="grouped")
-                copy = nc.scalar.copy
+        def biases():
+            nc.tensor.transpose(bias_t[:], bias_rows[:], ident[:])
+            nc.vector.tensor_copy(out=b1_col[:], in_=bias_t[:, 0:b1_rows])
+            nc.vector.tensor_copy(
+                out=b2_col[:], in_=bias_t[:, b1_rows : b1_rows + b2_rows].rearrange("p (n c) -> p c n", n=NB)
+            )
+
+        z_codes = [keep.tile([P, NB, P], U32, align_bytes=64, name="z_codes%d" % g) for g in range(G)]
+        z_scales = [keep.tile([P, NB, P], U8, align_bytes=64, name="z_scales%d" % g) for g in range(G)]
+        z_grouped = {}
+
+        def copy_z(g, pool, copy):
+            grouped = pool.tile([P, NB, P, PACK], BF16, align_bytes=64, tag="grouped")
             copy(
-                out=z_grouped[:].rearrange("p n r t -> p r t n"),
+                out=grouped[:].rearrange("p n r t -> p r t n"),
                 in_=y_raw[g][:].rearrange("p (t r n) -> p r t n", t=PACK, n=NB),
             )
-            b_cols = slice(g * P, (g + 1) * P)
-            for n in range(NB):
-                quantise(
-                    z_grouped[:, n, :, :].rearrange("p r t -> p (r t)"), z_codes[:, n, b_cols], z_scales[:, n, b_cols]
-                )
+            z_grouped[g] = grouped
+
+        def copy_z_v(g):
+            copy_z(g, by_vector, nc.vector.tensor_copy)
+
+        def copy_z_s(g):
+            copy_z(g, by_scalar, nc.scalar.copy)
+
+        def quantise_z(g):
+            quantise(
+                z_grouped[g][:].rearrange("p n r t -> p (n r t)"),
+                z_codes[g][:].rearrange("p n r -> p (n r)"),
+                z_scales[g][:].rearrange("p n r -> p (n r)"),
+            )
 
         w1_codes = [keep.tile([P, H], U32, align_bytes=64, name="w1_codes%d" % n) for n in range(NB)]
         w1_scales = [keep.tile([P, H], U8, align_bytes=64, name="w1_scales%d" % n) for n in range(NB)]
+        w1_grouped = {}
 
-        def prepare_w1(n):
-            for half, (pool, copy) in enumerate(
-                ((by_vector, nc.vector.tensor_copy), (by_scalar, nc.scalar.copy))
-            ):
-                j_cols = slice(half * HALF_H, (half + 1) * HALF_H)
-                w_grouped = pool.tile([P, HALF_H, PACK], BF16, align_bytes=64, tag="grouped")
-                regroup(copy, w_grouped[:], w1_raw[n][:, :, j_cols])
-                quantise(
-                    w_grouped[:].rearrange("p c t -> p (c t)"), w1_codes[n][:, j_cols], w1_scales[n][:, j_cols]
-                )
+        def copy_w1(n, half, pool, copy):
+            j_cols = slice(half * HALF_H, (half + 1) * HALF_H)
+            grouped = pool.tile([P, HALF_H, PACK], BF16, align_bytes=64, tag="grouped")
+            regroup(copy, grouped[:], w1_raw[n][:, :, j_cols])
+            w1_grouped[n, half] = grouped
 
-        w2_codes = [
-            [keep.tile([P, H_PASSES, HALF_I], U32, align_bytes=64, name="w2_codes%d_%d" % (half, n)) for n in range(NB)]
-            for half in range(2)
-        ]
-        w2_scales = [
-            [keep.tile([P, H_PASSES, HALF_I], U8, align_bytes=64, name="w2_scales%d_%d" % (half, n)) for n in range(NB)]
-            for half in range(2)
-        ]
+        def copy_w1_v(n, half):
+            copy_w1(n, half, by_vector, nc.vector.tensor_copy)
 
-        def prepare_w2(n, half, pool, copy):
-            i_cols = slice(half * HALF_I, (half + 1) * HALF_I)
-            w_grouped = pool.tile([P, H_PASSES, HALF_I, PACK], BF16, align_bytes=64, tag="grouped")
-            for s in range(H_PASSES):
-                regroup(copy, w_grouped[:, s, :, :], w2_raw[n][:, s, :, i_cols])
+        def copy_w1_s(n, half):
+            copy_w1(n, half, by_scalar, nc.scalar.copy)
+
+        def quantise_w1(n, half):
+            j_cols = slice(half * HALF_H, (half + 1) * HALF_H)
             quantise(
-                w_grouped[:].rearrange("p s c t -> p (s c t)"),
-                w2_codes[half][n][:].rearrange("p s c -> p (s c)"),
-                w2_scales[half][n][:].rearrange("p s c -> p (s c)"),
+                w1_grouped[n, half][:].rearrange("p c t -> p (c t)"), w1_codes[n][:, j_cols], w1_scales[n][:, j_cols]
             )
 
-        h_codes = [keep.tile([P, H_PASSES, BS], U32, align_bytes=64, name="h_codes%d" % n) for n in range(NB)]
-        h_scales = [keep.tile([P, H_PASSES, BS], U8, align_bytes=64, name="h_scales%d" % n) for n in range(NB)]
+        w2_low_codes = [keep.tile([P, H_PASSES, HALF_I], U32, align_bytes=64, name="w2_low_codes%d" % n) for n in range(NB)]
+        w2_low_scales = [keep.tile([P, H_PASSES, HALF_I], U8, align_bytes=64, name="w2_low_scales%d" % n) for n in range(NB)]
+        w2_high_codes = {
+            c: keep.tile([P, NB, H_PASSES, P], U32, align_bytes=64, name="w2_high_codes%d" % c) for c in (2, 3)
+        }
+        w2_high_scales = {
+            c: keep.tile([P, NB, H_PASSES, P], U8, align_bytes=64, name="w2_high_scales%d" % c) for c in (2, 3)
+        }
+        w2_grouped = {}
 
-        def first_layer(n):
+        def copy_w2_low(n):
+            grouped = by_vector.tile([P, H_PASSES, HALF_I, PACK], BF16, align_bytes=64, tag="grouped")
             for s in range(H_PASSES):
-                h_planes = hidden.tile([P, PACK, BS], BF16)
-                for t in range(PACK):
-                    chunk = s * PACK + t
-                    j_cols = slice(chunk * P, (chunk + 1) * P)
-                    h_acc = psum_h.tile([P, BS], F32)
-                    nc.tensor.matmul_mx(
-                        out=h_acc[:],
-                        lhsT=w1_codes[n][:, j_cols].bitcast(FP8X4),
-                        lhsT_scale=w1_scales[n][:, j_cols],
-                        rhs=z_codes[:, n, :].bitcast(FP8X4),
-                        rhs_scale=z_scales[:, n, :],
-                        start=True,
-                        stop=True,
-                    )
-                    bias_at = n * H_CHUNKS + chunk
-                    nc.scalar.activation(
-                        out=h_planes[:, t, :], in_=h_acc[:], func=GELU, bias=b1_col[:, bias_at : bias_at + 1], scale=1.0
-                    )
-                h_grouped = by_vector.tile([P, BS, PACK], BF16, align_bytes=64, tag="grouped")
-                regroup(nc.vector.tensor_copy, h_grouped[:], h_planes[:])
-                quantise(h_grouped[:].rearrange("p c t -> p (c t)"), h_codes[n][:, s, :], h_scales[n][:, s, :])
+                regroup(nc.vector.tensor_copy, grouped[:, s, :, :], w2_raw[n][:, s, :, 0:HALF_I])
+            w2_grouped["low", n] = grouped
+
+        def quantise_w2_low(n):
+            quantise(
+                w2_grouped["low", n][:].rearrange("p s c t -> p (s c t)"),
+                w2_low_codes[n][:].rearrange("p s c -> p (s c)"),
+                w2_low_scales[n][:].rearrange("p s c -> p (s c)"),
+            )
+
+        def copy_w2_high(c, pair):
+            grouped = by_scalar.tile([P, 2, H_PASSES, P, PACK], BF16, align_bytes=64, tag="grouped")
+            for u in range(2):
+                for s in range(H_PASSES):
+                    regroup(nc.scalar.copy, grouped[:, u, s, :, :], w2_raw[2 * pair + u][:, s, :, c * P : (c + 1) * P])
+            w2_grouped[c, pair] = grouped
+
+        def quantise_w2_high(c, pair):
+            ns = slice(2 * pair, 2 * pair + 2)
+            quantise(
+                w2_grouped[c, pair][:].rearrange("p n s c t -> p (n s c t)"),
+                w2_high_codes[c][:, ns, :, :].rearrange("p n s c -> p (n s c)"),
+                w2_high_scales[c][:, ns, :, :].rearrange("p n s c -> p (n s c)"),
+            )
+
+        def w2_operand(chunk, n, s):
+            if chunk < I_CHUNKS // 2:
+                i_cols = slice(chunk * P, (chunk + 1) * P)
+                return w2_low_codes[n][:, s, i_cols], w2_low_scales[n][:, s, i_cols]
+            return w2_high_codes[chunk][:, n, s, :], w2_high_scales[chunk][:, n, s, :]
+
+        h_codes = [
+            [keep.tile([P, H_PASSES, HB], U32, align_bytes=64, name="h_codes%d_%d" % (a, n)) for n in range(NB)]
+            for a in range(B_HALVES)
+        ]
+        h_scales = [
+            [keep.tile([P, H_PASSES, HB], U8, align_bytes=64, name="h_scales%d_%d" % (a, n)) for n in range(NB)]
+            for a in range(B_HALVES)
+        ]
+        h_planes = {}
+        h_grouped = {}
+
+        def first_layer(half, n):
+            planes = hidden.tile([P, PACK, H_PASSES, HB], BF16, tag="planes")
+            h_planes[half, n] = planes
+            for s in range(H_PASSES):
+                for pair in range(PACK // 2):
+                    h_acc = psum_h.tile([P, 2, HB], F32)
+                    for u in range(2):
+                        chunk = s * PACK + 2 * pair + u
+                        j_cols = slice(chunk * P, (chunk + 1) * P)
+                        for within in range(G_HALF):
+                            g = half * G_HALF + within
+                            nc.tensor.matmul_mx(
+                                out=h_acc[:, u, within * P : (within + 1) * P],
+                                lhsT=w1_codes[n][:, j_cols].bitcast(FP8X4),
+                                lhsT_scale=w1_scales[n][:, j_cols],
+                                rhs=z_codes[g][:, n, :].bitcast(FP8X4),
+                                rhs_scale=z_scales[g][:, n, :],
+                                start=True,
+                                stop=True,
+                            )
+                    for u in range(2):
+                        t = 2 * pair + u
+                        bias_at = n * H_CHUNKS + s * PACK + t
+                        nc.scalar.activation(
+                            out=planes[:, t, s, :],
+                            in_=h_acc[:, u, :],
+                            func=GELU,
+                            bias=b1_col[:, bias_at : bias_at + 1],
+                            scale=1.0,
+                        )
+
+        def copy_h(half, n):
+            grouped = by_vector.tile([P, H_PASSES * HB, PACK], BF16, align_bytes=64, tag="grouped")
+            regroup(nc.vector.tensor_copy, grouped[:], h_planes[half, n][:].rearrange("p t s b -> p t (s b)"))
+            h_grouped[half, n] = grouped
+
+        def quantise_h(half, n):
+            quantise(
+                h_grouped[half, n][:].rearrange("p c t -> p (c t)"),
+                h_codes[half][n][:].rearrange("p s b -> p (s b)"),
+                h_scales[half][n][:].rearrange("p s b -> p (s b)"),
+            )
 
         def second_layer(chunk, g):
-            half, within = divmod(chunk, I_CHUNKS // 2)
-            i_cols = slice(within * P, (within + 1) * P)
-            b_cols = slice(g * P, (g + 1) * P)
+            b_half, b_within = divmod(g, G_HALF)
+            b_cols = slice(b_within * P, (b_within + 1) * P)
             o_acc = psum_o.tile([P, NB, P], F32)
             for n in range(NB):
                 for s in range(H_PASSES):
+                    codes, scales = w2_operand(chunk, n, s)
                     nc.tensor.matmul_mx(
                         out=o_acc[:, n, :],
-                        lhsT=w2_codes[half][n][:, s, i_cols].bitcast(FP8X4),
-                        lhsT_scale=w2_scales[half][n][:, s, i_cols],
-                        rhs=h_codes[n][:, s, b_cols].bitcast(FP8X4),
-                        rhs_scale=h_scales[n][:, s, b_cols],
+                        lhsT=codes.bitcast(FP8X4),
+                        lhsT_scale=scales,
+                        rhs=h_codes[b_half][n][:, s, b_cols].bitcast(FP8X4),
+                        rhs_scale=h_scales[b_half][n][:, s, b_cols],
                         start=(s == 0),
                         stop=(s == H_PASSES - 1),
                     )
@@ -202,16 +283,82 @@ def tile_blockmlp_mixerblock_pa_kernel(tc, y0, W1, b1, W2, b2, out):
                 out=out_rows[g, chunk * P : (chunk + 1) * P, :], in_=o_rows[:].rearrange("p r n -> p (r n)")
             )
 
-        prepare_w1(0)
-        for n in range(NB):
-            if n + 1 < NB:
-                prepare_w1(n + 1)
-            first_layer(n)
-            prepare_w2(n, 0, by_vector, nc.vector.tensor_copy)
-        for half in range(2):
-            if half == 1:
-                for n in range(NB):
-                    prepare_w2(n, 1, by_scalar, nc.scalar.copy)
-            for within in range(I_CHUNKS // 2):
-                for g in range(G):
-                    second_layer(half * (I_CHUNKS // 2) + within, g)
+        copy_z_v(0)
+        copy_z_s(1)
+        quantise_z(0)
+        copy_w1_v(0, 0)
+        copy_w1_s(0, 1)
+        quantise_z(1)
+        quantise_w1(0, 0)
+        biases()
+        copy_w1_v(1, 0)
+        copy_w1_s(1, 1)
+        quantise_w1(0, 1)
+        quantise_w1(1, 0)
+        first_layer(0, 0)
+        copy_w1_v(2, 0)
+        copy_w1_s(2, 1)
+        quantise_w1(1, 1)
+        quantise_w1(2, 0)
+        first_layer(0, 1)
+        copy_w1_v(3, 0)
+        copy_w1_s(3, 1)
+        copy_h(0, 0)
+        quantise_w1(3, 0)
+        quantise_h(0, 0)
+        quantise_w1(2, 1)
+        first_layer(0, 2)
+        copy_w2_low(0)
+        copy_z_s(3)
+        copy_h(0, 1)
+        quantise_w2_low(0)
+        quantise_h(0, 1)
+        quantise_w1(3, 1)
+        first_layer(0, 3)
+        copy_z_v(2)
+        copy_h(0, 2)
+        quantise_z(2)
+        quantise_z(3)
+        quantise_h(0, 2)
+        first_layer(1, 0)
+        copy_w2_low(1)
+        copy_h(0, 3)
+        quantise_w2_low(1)
+        copy_w2_low(2)
+        quantise_h(0, 3)
+        first_layer(1, 1)
+        copy_h(1, 0)
+        quantise_w2_low(2)
+        copy_w2_low(3)
+        quantise_h(1, 0)
+        quantise_w2_low(3)
+        first_layer(1, 2)
+        copy_h(1, 1)
+        second_layer(0, 0)
+        quantise_h(1, 1)
+        first_layer(1, 3)
+        second_layer(0, 1)
+        copy_w2_high(2, 0)
+        copy_h(1, 2)
+        second_layer(1, 0)
+        second_layer(1, 1)
+        quantise_h(1, 2)
+        copy_w2_high(2, 1)
+        copy_h(1, 3)
+        quantise_w2_high(2, 0)
+        quantise_h(1, 3)
+        second_layer(0, 2)
+        second_layer(0, 3)
+        copy_w2_high(3, 0)
+        quantise_w2_high(2, 1)
+        second_layer(1, 2)
+        second_layer(1, 3)
+        copy_w2_high(3, 1)
+        second_layer(2, 0)
+        second_layer(2, 1)
+        quantise_w2_high(3, 0)
+        second_layer(2, 2)
+        second_layer(2, 3)
+        quantise_w2_high(3, 1)
+        for g in range(G):
+            second_layer(3, g)

@@ -21,11 +21,8 @@ H_CHUNKS = H // P
 H_PASSES = H // K_PASS
 I_CHUNKS = BD // P
 HALF_H = H // 2
-HALF_I = BD // 2
-B_HALVES = 2
-HB = BS // B_HALVES
-G_HALF = G // B_HALVES
-RUN = 4
+BANK = 1024
+RUN = 8
 
 FLOPS = 2 * BS * NB * (BD * H + H * BD)
 
@@ -50,8 +47,8 @@ def tile_blockmlp_mixerblock_pa_kernel(tc, y0, W1, b1, W2, b2, out):
         by_scalar = ctx.enter_context(tc.tile_pool(name="by_scalar", bufs=4))
         hidden = ctx.enter_context(tc.tile_pool(name="hidden", bufs=4))
         results = ctx.enter_context(tc.tile_pool(name="results", bufs=6))
-        psum_bias = ctx.enter_context(tc.psum_pool(name="psum_bias", bufs=1))
-        psum_h = ctx.enter_context(tc.psum_pool(name="psum_h", bufs=4))
+        psum_relay = ctx.enter_context(tc.psum_pool(name="psum_relay", bufs=2))
+        psum_h = ctx.enter_context(tc.psum_pool(name="psum_h", bufs=3))
         psum_o = ctx.enter_context(tc.psum_pool(name="psum_o", bufs=3))
         ctx.enter_context(tc.manual_schedule())
 
@@ -82,8 +79,8 @@ def tile_blockmlp_mixerblock_pa_kernel(tc, y0, W1, b1, W2, b2, out):
                 out=w2_raw[n][:], in_=W2[n].rearrange("(s t p) i -> p s t i", s=H_PASSES, t=PACK)
             )
 
-        load_y(0)
-        load_y(1)
+        for g in range(G):
+            load_y(g)
         nc.sync.dma_start(out=bias_rows[0:b1_rows, :], in_=b1.rearrange("n o (c p) -> (n o c) p", p=P))
         nc.sync.dma_start(
             out=bias_rows[b1_rows : b1_rows + b2_rows, :], in_=b2.rearrange("n o (c p) -> (n o c) p", p=P)
@@ -91,20 +88,16 @@ def tile_blockmlp_mixerblock_pa_kernel(tc, y0, W1, b1, W2, b2, out):
         for n in range(NB):
             for half in range(2):
                 load_w1(n, half)
-        load_w2(0)
-        load_w2(1)
-        load_y(2)
-        load_y(3)
-        load_w2(2)
-        load_w2(3)
+        for n in range(NB):
+            load_w2(n)
 
         ident = keep.tile([P, P], BF16)
         make_identity(nc, ident[:])
-        bias_t = psum_bias.tile([P, P], BF16)
         b1_col = keep.tile([P, b1_rows], F32)
         b2_col = keep.tile([P, I_CHUNKS, NB], F32)
 
         def biases():
+            bias_t = psum_relay.tile([P, P], BF16, tag="relay")
             nc.tensor.transpose(bias_t[:], bias_rows[:], ident[:])
             nc.vector.tensor_copy(out=b1_col[:], in_=bias_t[:, 0:b1_rows])
             nc.vector.tensor_copy(
@@ -136,139 +129,123 @@ def tile_blockmlp_mixerblock_pa_kernel(tc, y0, W1, b1, W2, b2, out):
                 z_scales[g][:].rearrange("p n r -> p (n r)"),
             )
 
+        def relay(grouped_flat, parts):
+            bank = psum_relay.tile([P, BANK], BF16, tag="relay")
+            for u, planes in enumerate(parts):
+                nc.tensor.matmul(
+                    out=bank[:, u * K_PASS : (u + 1) * K_PASS].rearrange("p (c t) -> p c t", t=PACK),
+                    lhsT=ident[:],
+                    rhs=planes.rearrange("p t c -> p c t"),
+                    start=True,
+                    stop=True,
+                )
+            nc.scalar.copy(out=grouped_flat, in_=bank[:])
+
         w1_codes = [keep.tile([P, H], U32, align_bytes=64, name="w1_codes%d" % n) for n in range(NB)]
         w1_scales = [keep.tile([P, H], U8, align_bytes=64, name="w1_scales%d" % n) for n in range(NB)]
         w1_grouped = {}
 
-        def copy_w1(n, half, pool, copy):
-            j_cols = slice(half * HALF_H, (half + 1) * HALF_H)
-            grouped = pool.tile([P, HALF_H, PACK], BF16, align_bytes=64, tag="grouped")
-            regroup(copy, grouped[:], w1_raw[n][:, :, j_cols])
-            w1_grouped[n, half] = grouped
+        def copy_w1_low(n):
+            grouped = by_vector.tile([P, HALF_H, PACK], BF16, align_bytes=64, tag="grouped")
+            regroup(nc.vector.tensor_copy, grouped[:], w1_raw[n][:, :, 0:HALF_H])
+            w1_grouped[n, 0] = grouped
 
-        def copy_w1_v(n, half):
-            copy_w1(n, half, by_vector, nc.vector.tensor_copy)
-
-        def copy_w1_s(n, half):
-            copy_w1(n, half, by_scalar, nc.scalar.copy)
+        def copy_w1_high(n):
+            grouped = by_scalar.tile([P, 2, BANK], BF16, align_bytes=64, tag="grouped")
+            for u in range(2):
+                j0 = HALF_H + 2 * u * P
+                relay(grouped[:, u, :], [w1_raw[n][:, :, j : j + P] for j in (j0, j0 + P)])
+            w1_grouped[n, 1] = grouped
 
         def quantise_w1(n, half):
             j_cols = slice(half * HALF_H, (half + 1) * HALF_H)
             quantise(
-                w1_grouped[n, half][:].rearrange("p c t -> p (c t)"), w1_codes[n][:, j_cols], w1_scales[n][:, j_cols]
+                (w1_grouped[n, half][:].rearrange("p c t -> p (c t)")), w1_codes[n][:, j_cols], w1_scales[n][:, j_cols]
             )
 
-        w2_low_codes = [keep.tile([P, H_PASSES, HALF_I], U32, align_bytes=64, name="w2_low_codes%d" % n) for n in range(NB)]
-        w2_low_scales = [keep.tile([P, H_PASSES, HALF_I], U8, align_bytes=64, name="w2_low_scales%d" % n) for n in range(NB)]
-        w2_high_codes = {
-            c: keep.tile([P, NB, H_PASSES, P], U32, align_bytes=64, name="w2_high_codes%d" % c) for c in (2, 3)
-        }
-        w2_high_scales = {
-            c: keep.tile([P, NB, H_PASSES, P], U8, align_bytes=64, name="w2_high_scales%d" % c) for c in (2, 3)
-        }
+        w2_codes = [keep.tile([P, NB, H_PASSES, P], U32, align_bytes=64, name="w2_codes%d" % c) for c in range(I_CHUNKS)]
+        w2_scales = [keep.tile([P, NB, H_PASSES, P], U8, align_bytes=64, name="w2_scales%d" % c) for c in range(I_CHUNKS)]
         w2_grouped = {}
 
-        def copy_w2_low(n):
-            grouped = by_vector.tile([P, H_PASSES, HALF_I, PACK], BF16, align_bytes=64, tag="grouped")
-            for s in range(H_PASSES):
-                regroup(nc.vector.tensor_copy, grouped[:, s, :, :], w2_raw[n][:, s, :, 0:HALF_I])
-            w2_grouped["low", n] = grouped
+        def w2_part(c, n, s):
+            return w2_raw[n][:, s, :, c * P : (c + 1) * P]
 
-        def quantise_w2_low(n):
-            quantise(
-                w2_grouped["low", n][:].rearrange("p s c t -> p (s c t)"),
-                w2_low_codes[n][:].rearrange("p s c -> p (s c)"),
-                w2_low_scales[n][:].rearrange("p s c -> p (s c)"),
-            )
-
-        def copy_w2_high(c, pair):
-            grouped = by_scalar.tile([P, 2, H_PASSES, P, PACK], BF16, align_bytes=64, tag="grouped")
+        def copy_w2(c, pair, pool, copy):
+            grouped = pool.tile([P, 2, H_PASSES, P, PACK], BF16, align_bytes=64, tag="grouped")
             for u in range(2):
                 for s in range(H_PASSES):
-                    regroup(nc.scalar.copy, grouped[:, u, s, :, :], w2_raw[2 * pair + u][:, s, :, c * P : (c + 1) * P])
+                    regroup(copy, grouped[:, u, s, :, :], w2_part(c, 2 * pair + u, s))
             w2_grouped[c, pair] = grouped
 
-        def quantise_w2_high(c, pair):
+        def copy_w2_s(c, pair):
+            copy_w2(c, pair, by_scalar, nc.scalar.copy)
+
+        def copy_w2_v(c, pair):
+            copy_w2(c, pair, by_vector, nc.vector.tensor_copy)
+
+        def copy_w2_relay(c, pair):
+            grouped = by_scalar.tile([P, 2, H_PASSES, P, PACK], BF16, align_bytes=64, tag="grouped")
+            for u in range(2):
+                relay(
+                    grouped[:, u, :, :, :].rearrange("p s c t -> p (s c t)"),
+                    [w2_part(c, 2 * pair + u, s) for s in range(H_PASSES)],
+                )
+            w2_grouped[c, pair] = grouped
+
+        def quantise_w2(c, pair):
             ns = slice(2 * pair, 2 * pair + 2)
             quantise(
                 w2_grouped[c, pair][:].rearrange("p n s c t -> p (n s c t)"),
-                w2_high_codes[c][:, ns, :, :].rearrange("p n s c -> p (n s c)"),
-                w2_high_scales[c][:, ns, :, :].rearrange("p n s c -> p (n s c)"),
+                w2_codes[c][:, ns, :, :].rearrange("p n s c -> p (n s c)"),
+                w2_scales[c][:, ns, :, :].rearrange("p n s c -> p (n s c)"),
             )
 
-        def w2_operand(chunk, n, s):
-            if chunk < I_CHUNKS // 2:
-                i_cols = slice(chunk * P, (chunk + 1) * P)
-                return w2_low_codes[n][:, s, i_cols], w2_low_scales[n][:, s, i_cols]
-            return w2_high_codes[chunk][:, n, s, :], w2_high_scales[chunk][:, n, s, :]
-
-        h_codes = [
-            [keep.tile([P, H_PASSES, HB], U32, align_bytes=64, name="h_codes%d_%d" % (a, n)) for n in range(NB)]
-            for a in range(B_HALVES)
-        ]
-        h_scales = [
-            [keep.tile([P, H_PASSES, HB], U8, align_bytes=64, name="h_scales%d_%d" % (a, n)) for n in range(NB)]
-            for a in range(B_HALVES)
-        ]
+        h_codes = [keep.tile([P, H_PASSES, BS], U32, align_bytes=64, name="h_codes%d" % n) for n in range(NB)]
+        h_scales = [keep.tile([P, H_PASSES, BS], U8, align_bytes=64, name="h_scales%d" % n) for n in range(NB)]
         h_planes = {}
         h_grouped = {}
 
-        def first_layer(half, n):
-            planes = hidden.tile([P, PACK, H_PASSES, HB], BF16, tag="planes")
-            h_planes[half, n] = planes
-            for s in range(H_PASSES):
-                for pair in range(PACK // 2):
-                    h_acc = psum_h.tile([P, 2, HB], F32)
-                    for u in range(2):
-                        chunk = s * PACK + 2 * pair + u
-                        j_cols = slice(chunk * P, (chunk + 1) * P)
-                        for within in range(G_HALF):
-                            g = half * G_HALF + within
-                            nc.tensor.matmul_mx(
-                                out=h_acc[:, u, within * P : (within + 1) * P],
-                                lhsT=w1_codes[n][:, j_cols].bitcast(FP8X4),
-                                lhsT_scale=w1_scales[n][:, j_cols],
-                                rhs=z_codes[g][:, n, :].bitcast(FP8X4),
-                                rhs_scale=z_scales[g][:, n, :],
-                                start=True,
-                                stop=True,
-                            )
-                    for u in range(2):
-                        t = 2 * pair + u
-                        bias_at = n * H_CHUNKS + s * PACK + t
-                        nc.scalar.activation(
-                            out=planes[:, t, s, :],
-                            in_=h_acc[:, u, :],
-                            func=GELU,
-                            bias=b1_col[:, bias_at : bias_at + 1],
-                            scale=1.0,
-                        )
+        def first_layer(n, s):
+            planes = hidden.tile([P, PACK, BS], BF16, tag="planes")
+            h_planes[n, s] = planes
+            for t in range(PACK):
+                chunk = s * PACK + t
+                j_cols = slice(chunk * P, (chunk + 1) * P)
+                h_acc = psum_h.tile([P, BS], F32)
+                for g in range(G):
+                    nc.tensor.matmul_mx(
+                        out=h_acc[:, g * P : (g + 1) * P],
+                        lhsT=w1_codes[n][:, j_cols].bitcast(FP8X4),
+                        lhsT_scale=w1_scales[n][:, j_cols],
+                        rhs=z_codes[g][:, n, :].bitcast(FP8X4),
+                        rhs_scale=z_scales[g][:, n, :],
+                        start=True,
+                        stop=True,
+                    )
+                bias_at = n * H_CHUNKS + chunk
+                nc.scalar.activation(
+                    out=planes[:, t, :], in_=h_acc[:], func=GELU, bias=b1_col[:, bias_at : bias_at + 1], scale=1.0
+                )
 
-        def copy_h(half, n):
-            grouped = by_vector.tile([P, H_PASSES * HB, PACK], BF16, align_bytes=64, tag="grouped")
-            regroup(nc.vector.tensor_copy, grouped[:], h_planes[half, n][:].rearrange("p t s b -> p t (s b)"))
-            h_grouped[half, n] = grouped
+        def copy_h(n, s):
+            grouped = by_vector.tile([P, BS, PACK], BF16, align_bytes=64, tag="grouped")
+            regroup(nc.vector.tensor_copy, grouped[:], h_planes[n, s][:])
+            h_grouped[n, s] = grouped
 
-        def quantise_h(half, n):
-            quantise(
-                h_grouped[half, n][:].rearrange("p c t -> p (c t)"),
-                h_codes[half][n][:].rearrange("p s b -> p (s b)"),
-                h_scales[half][n][:].rearrange("p s b -> p (s b)"),
-            )
+        def quantise_h(n, s):
+            quantise(h_grouped[n, s][:].rearrange("p c t -> p (c t)"), h_codes[n][:, s, :], h_scales[n][:, s, :])
 
         def second_layer(chunk, g):
-            b_half, b_within = divmod(g, G_HALF)
-            b_cols = slice(b_within * P, (b_within + 1) * P)
+            b_cols = slice(g * P, (g + 1) * P)
             o_acc = psum_o.tile([P, NB, P], F32)
             for n in range(NB):
                 for s in range(H_PASSES):
-                    codes, scales = w2_operand(chunk, n, s)
                     nc.tensor.matmul_mx(
                         out=o_acc[:, n, :],
-                        lhsT=codes.bitcast(FP8X4),
-                        lhsT_scale=scales,
-                        rhs=h_codes[b_half][n][:, s, b_cols].bitcast(FP8X4),
-                        rhs_scale=h_scales[b_half][n][:, s, b_cols],
+                        lhsT=w2_codes[chunk][:, n, s, :].bitcast(FP8X4),
+                        lhsT_scale=w2_scales[chunk][:, n, s, :],
+                        rhs=h_codes[n][:, s, b_cols].bitcast(FP8X4),
+                        rhs_scale=h_scales[n][:, s, b_cols],
                         start=(s == 0),
                         stop=(s == H_PASSES - 1),
                     )
@@ -286,79 +263,75 @@ def tile_blockmlp_mixerblock_pa_kernel(tc, y0, W1, b1, W2, b2, out):
         copy_z_v(0)
         copy_z_s(1)
         quantise_z(0)
-        copy_w1_v(0, 0)
-        copy_w1_s(0, 1)
+        copy_z_v(2)
+        copy_z_s(3)
         quantise_z(1)
+        copy_w1_low(0)
+        copy_w1_high(0)
+        quantise_z(2)
         quantise_w1(0, 0)
         biases()
-        copy_w1_v(1, 0)
-        copy_w1_s(1, 1)
-        quantise_w1(0, 1)
-        quantise_w1(1, 0)
-        first_layer(0, 0)
-        copy_w1_v(2, 0)
-        copy_w1_s(2, 1)
-        quantise_w1(1, 1)
-        quantise_w1(2, 0)
-        first_layer(0, 1)
-        copy_w1_v(3, 0)
-        copy_w1_s(3, 1)
-        copy_h(0, 0)
-        quantise_w1(3, 0)
-        quantise_h(0, 0)
-        quantise_w1(2, 1)
-        first_layer(0, 2)
-        copy_w2_low(0)
-        copy_z_s(3)
-        copy_h(0, 1)
-        quantise_w2_low(0)
-        quantise_h(0, 1)
-        quantise_w1(3, 1)
-        first_layer(0, 3)
-        copy_z_v(2)
-        copy_h(0, 2)
-        quantise_z(2)
         quantise_z(3)
-        quantise_h(0, 2)
+        copy_w1_high(1)
+        first_layer(0, 0)
+        quantise_w1(0, 1)
+        copy_w1_low(1)
+        first_layer(0, 1)
+        copy_w1_high(2)
+        quantise_w1(1, 1)
+        quantise_w1(1, 0)
+        copy_w1_low(2)
         first_layer(1, 0)
-        copy_w2_low(1)
-        copy_h(0, 3)
-        quantise_w2_low(1)
-        copy_w2_low(2)
-        quantise_h(0, 3)
+        copy_h(0, 0)
+        quantise_w1(2, 0)
+        quantise_h(0, 0)
         first_layer(1, 1)
+        copy_w1_high(3)
+        copy_h(0, 1)
+        quantise_w1(2, 1)
+        quantise_h(0, 1)
+        copy_w1_low(3)
+        first_layer(2, 0)
         copy_h(1, 0)
-        quantise_w2_low(2)
-        copy_w2_low(3)
+        quantise_w1(3, 0)
         quantise_h(1, 0)
-        quantise_w2_low(3)
-        first_layer(1, 2)
+        first_layer(2, 1)
+        copy_w2_relay(0, 0)
         copy_h(1, 1)
-        second_layer(0, 0)
+        copy_w2_v(1, 1)
+        quantise_w1(3, 1)
         quantise_h(1, 1)
-        first_layer(1, 3)
-        second_layer(0, 1)
-        copy_w2_high(2, 0)
-        copy_h(1, 2)
-        second_layer(1, 0)
-        second_layer(1, 1)
-        quantise_h(1, 2)
-        copy_w2_high(2, 1)
-        copy_h(1, 3)
-        quantise_w2_high(2, 0)
-        quantise_h(1, 3)
-        second_layer(0, 2)
-        second_layer(0, 3)
-        copy_w2_high(3, 0)
-        quantise_w2_high(2, 1)
-        second_layer(1, 2)
-        second_layer(1, 3)
-        copy_w2_high(3, 1)
+        first_layer(3, 0)
+        copy_w2_relay(0, 1)
+        copy_h(2, 0)
+        quantise_w2(0, 0)
+        quantise_h(2, 0)
+        first_layer(3, 1)
+        copy_w2_s(1, 0)
+        copy_h(2, 1)
+        quantise_w2(0, 1)
+        quantise_h(2, 1)
+        copy_h(3, 0)
+        quantise_w2(1, 1)
+        quantise_h(3, 0)
+        copy_w2_s(2, 0)
+        copy_h(3, 1)
+        copy_w2_s(2, 1)
+        copy_w2_s(3, 0)
+        copy_w2_s(3, 1)
+        quantise_h(3, 1)
+        quantise_w2(1, 0)
+        for g in range(G):
+            second_layer(0, g)
+        quantise_w2(2, 0)
+        for g in range(G):
+            second_layer(1, g)
+        quantise_w2(2, 1)
         second_layer(2, 0)
         second_layer(2, 1)
-        quantise_w2_high(3, 0)
+        quantise_w2(3, 0)
         second_layer(2, 2)
+        quantise_w2(3, 1)
         second_layer(2, 3)
-        quantise_w2_high(3, 1)
         for g in range(G):
             second_layer(3, g)

@@ -68,11 +68,8 @@ def tile_blockmlp_mixerblock_pa_kernel(tc, y0, W1, b1, W2, b2, out):
         def load_y(g):
             nc.sync.dma_start(out=y_raw[g][:], in_=y0[g * P : (g + 1) * P, :])
 
-        def load_w1(n, half):
-            j_cols = slice(half * HALF_H, (half + 1) * HALF_H)
-            nc.sync.dma_start(
-                out=w1_raw[n][:, :, j_cols], in_=W1[n][:, j_cols].rearrange("(p t) j -> p t j", t=PACK)
-            )
+        def load_w1(n):
+            nc.sync.dma_start(out=w1_raw[n][:], in_=W1[n].rearrange("(p t) j -> p t j", t=PACK))
 
         def load_w2(n):
             nc.sync.dma_start(
@@ -86,8 +83,7 @@ def tile_blockmlp_mixerblock_pa_kernel(tc, y0, W1, b1, W2, b2, out):
             out=bias_rows[b1_rows : b1_rows + b2_rows, :], in_=b2.rearrange("n o (c p) -> (n o c) p", p=P)
         )
         for n in range(NB):
-            for half in range(2):
-                load_w1(n, half)
+            load_w1(n)
         for n in range(NB):
             load_w2(n)
 
@@ -104,8 +100,8 @@ def tile_blockmlp_mixerblock_pa_kernel(tc, y0, W1, b1, W2, b2, out):
                 out=b2_col[:], in_=bias_t[:, b1_rows : b1_rows + b2_rows].rearrange("p (n c) -> p c n", n=NB)
             )
 
-        z_codes = [keep.tile([P, NB, P], U32, align_bytes=64, name="z_codes%d" % g) for g in range(G)]
-        z_scales = [keep.tile([P, NB, P], U8, align_bytes=64, name="z_scales%d" % g) for g in range(G)]
+        z_codes = keep.tile([P, NB, BS], U32, align_bytes=64)
+        z_scales = keep.tile([P, NB, BS], U8, align_bytes=64)
         z_grouped = {}
 
         def copy_z(g, pool, copy):
@@ -123,23 +119,22 @@ def tile_blockmlp_mixerblock_pa_kernel(tc, y0, W1, b1, W2, b2, out):
             copy_z(g, by_scalar, nc.scalar.copy)
 
         def quantise_z(g):
-            quantise(
-                z_grouped[g][:].rearrange("p n r t -> p (n r t)"),
-                z_codes[g][:].rearrange("p n r -> p (n r)"),
-                z_scales[g][:].rearrange("p n r -> p (n r)"),
+            b_cols = slice(g * P, (g + 1) * P)
+            for n in range(NB):
+                quantise(
+                    z_grouped[g][:, n, :, :].rearrange("p r t -> p (r t)"), z_codes[:, n, b_cols], z_scales[:, n, b_cols]
+                )
+
+        def relay_part(bank_part, planes):
+            nc.tensor.matmul(
+                out=bank_part.rearrange("p c t -> p t c"), lhsT=ident[:], rhs=planes, start=True, stop=True
             )
 
-        def relay(grouped_flat, parts):
-            bank = psum_relay.tile([P, BANK], BF16, tag="relay")
-            for u, planes in enumerate(parts):
-                nc.tensor.matmul(
-                    out=bank[:, u * K_PASS : (u + 1) * K_PASS].rearrange("p (c t) -> p c t", t=PACK),
-                    lhsT=ident[:],
-                    rhs=planes.rearrange("p t c -> p c t"),
-                    start=True,
-                    stop=True,
-                )
-            nc.scalar.copy(out=grouped_flat, in_=bank[:])
+        def relay(grouped, planes):
+            bank = psum_relay.tile([P, BANK // K_PASS, P, PACK], BF16, tag="relay")
+            for u in range(BANK // K_PASS):
+                relay_part(bank[:, u, :, :], planes[:, :, u * P : (u + 1) * P])
+            nc.scalar.copy(out=grouped.rearrange("p c t -> p (c t)"), in_=bank[:].rearrange("p u c t -> p (u c t)"))
 
         w1_codes = [keep.tile([P, H], U32, align_bytes=64, name="w1_codes%d" % n) for n in range(NB)]
         w1_scales = [keep.tile([P, H], U8, align_bytes=64, name="w1_scales%d" % n) for n in range(NB)]
@@ -150,12 +145,13 @@ def tile_blockmlp_mixerblock_pa_kernel(tc, y0, W1, b1, W2, b2, out):
             regroup(nc.vector.tensor_copy, grouped[:], w1_raw[n][:, :, 0:HALF_H])
             w1_grouped[n, 0] = grouped
 
-        def copy_w1_high(n):
-            grouped = by_scalar.tile([P, 2, BANK], BF16, align_bytes=64, tag="grouped")
-            for u in range(2):
-                j0 = HALF_H + 2 * u * P
-                relay(grouped[:, u, :], [w1_raw[n][:, :, j : j + P] for j in (j0, j0 + P)])
-            w1_grouped[n, 1] = grouped
+        def relay_w1(n, half):
+            grouped = by_scalar.tile([P, HALF_H, PACK], BF16, align_bytes=64, tag="grouped")
+            width = BANK // PACK
+            for c in range(0, HALF_H, width):
+                j0 = half * HALF_H + c
+                relay(grouped[:, c : c + width, :], w1_raw[n][:, :, j0 : j0 + width])
+            w1_grouped[n, half] = grouped
 
         def quantise_w1(n, half):
             j_cols = slice(half * HALF_H, (half + 1) * HALF_H)
@@ -183,12 +179,15 @@ def tile_blockmlp_mixerblock_pa_kernel(tc, y0, W1, b1, W2, b2, out):
         def copy_w2_v(c, pair):
             copy_w2(c, pair, by_vector, nc.vector.tensor_copy)
 
-        def copy_w2_relay(c, pair):
+        def relay_w2(c, pair):
             grouped = by_scalar.tile([P, 2, H_PASSES, P, PACK], BF16, align_bytes=64, tag="grouped")
             for u in range(2):
-                relay(
-                    grouped[:, u, :, :, :].rearrange("p s c t -> p (s c t)"),
-                    [w2_part(c, 2 * pair + u, s) for s in range(H_PASSES)],
+                bank = psum_relay.tile([P, H_PASSES, P, PACK], BF16, tag="relay")
+                for s in range(H_PASSES):
+                    relay_part(bank[:, s, :, :], w2_part(c, 2 * pair + u, s))
+                nc.scalar.copy(
+                    out=grouped[:, u, :, :, :].rearrange("p s c t -> p (s c t)"),
+                    in_=bank[:].rearrange("p s c t -> p (s c t)"),
                 )
             w2_grouped[c, pair] = grouped
 
@@ -212,16 +211,15 @@ def tile_blockmlp_mixerblock_pa_kernel(tc, y0, W1, b1, W2, b2, out):
                 chunk = s * PACK + t
                 j_cols = slice(chunk * P, (chunk + 1) * P)
                 h_acc = psum_h.tile([P, BS], F32)
-                for g in range(G):
-                    nc.tensor.matmul_mx(
-                        out=h_acc[:, g * P : (g + 1) * P],
-                        lhsT=w1_codes[n][:, j_cols].bitcast(FP8X4),
-                        lhsT_scale=w1_scales[n][:, j_cols],
-                        rhs=z_codes[g][:, n, :].bitcast(FP8X4),
-                        rhs_scale=z_scales[g][:, n, :],
-                        start=True,
-                        stop=True,
-                    )
+                nc.tensor.matmul_mx(
+                    out=h_acc[:],
+                    lhsT=w1_codes[n][:, j_cols].bitcast(FP8X4),
+                    lhsT_scale=w1_scales[n][:, j_cols],
+                    rhs=z_codes[:, n, :].bitcast(FP8X4),
+                    rhs_scale=z_scales[:, n, :],
+                    start=True,
+                    stop=True,
+                )
                 bias_at = n * H_CHUNKS + chunk
                 nc.scalar.activation(
                     out=planes[:, t, :], in_=h_acc[:], func=GELU, bias=b1_col[:, bias_at : bias_at + 1], scale=1.0
@@ -267,62 +265,64 @@ def tile_blockmlp_mixerblock_pa_kernel(tc, y0, W1, b1, W2, b2, out):
         copy_z_s(3)
         quantise_z(1)
         copy_w1_low(0)
-        copy_w1_high(0)
+        relay_w1(0, 1)
         quantise_z(2)
         quantise_w1(0, 0)
         biases()
         quantise_z(3)
-        copy_w1_high(1)
         first_layer(0, 0)
         quantise_w1(0, 1)
         copy_w1_low(1)
+        relay_w1(1, 1)
         first_layer(0, 1)
-        copy_w1_high(2)
-        quantise_w1(1, 1)
         quantise_w1(1, 0)
         copy_w1_low(2)
+        quantise_w1(1, 1)
+        relay_w1(2, 1)
         first_layer(1, 0)
         copy_h(0, 0)
         quantise_w1(2, 0)
         quantise_h(0, 0)
+        copy_w1_low(3)
         first_layer(1, 1)
-        copy_w1_high(3)
         copy_h(0, 1)
         quantise_w1(2, 1)
         quantise_h(0, 1)
-        copy_w1_low(3)
+        relay_w1(3, 1)
         first_layer(2, 0)
-        copy_h(1, 0)
         quantise_w1(3, 0)
+        copy_h(1, 0)
+        copy_w2_v(0, 0)
         quantise_h(1, 0)
-        first_layer(2, 1)
-        copy_w2_relay(0, 0)
-        copy_h(1, 1)
-        copy_w2_v(1, 1)
         quantise_w1(3, 1)
-        quantise_h(1, 1)
-        first_layer(3, 0)
-        copy_w2_relay(0, 1)
-        copy_h(2, 0)
+        first_layer(2, 1)
+        copy_h(1, 1)
         quantise_w2(0, 0)
+        quantise_h(1, 1)
+        copy_w2_v(0, 1)
+        first_layer(3, 0)
+        copy_h(2, 0)
+        quantise_w2(0, 1)
         quantise_h(2, 0)
         first_layer(3, 1)
-        copy_w2_s(1, 0)
+        relay_w2(1, 0)
+        relay_w2(1, 1)
         copy_h(2, 1)
-        quantise_w2(0, 1)
         quantise_h(2, 1)
-        copy_h(3, 0)
-        quantise_w2(1, 1)
-        quantise_h(3, 0)
         copy_w2_s(2, 0)
-        copy_h(3, 1)
+        copy_h(3, 0)
+        quantise_w2(1, 0)
         copy_w2_s(2, 1)
+        quantise_h(3, 0)
+        copy_h(3, 1)
+        quantise_w2(1, 1)
         copy_w2_s(3, 0)
         copy_w2_s(3, 1)
         quantise_h(3, 1)
-        quantise_w2(1, 0)
-        for g in range(G):
-            second_layer(0, g)
+        second_layer(0, 0)
+        second_layer(0, 1)
+        second_layer(0, 2)
+        second_layer(0, 3)
         quantise_w2(2, 0)
         for g in range(G):
             second_layer(1, g)

@@ -21,7 +21,6 @@ H_CHUNKS = H // P
 H_PASSES = H // K_PASS
 I_CHUNKS = BD // P
 HALF_H = H // 2
-BANK = 1024
 RUN = 8
 
 FLOPS = 2 * BS * NB * (BD * H + H * BD)
@@ -47,10 +46,9 @@ def tile_blockmlp_mixerblock_pa_kernel(tc, y0, W1, b1, W2, b2, out):
         by_scalar = ctx.enter_context(tc.tile_pool(name="by_scalar", bufs=4))
         hidden = ctx.enter_context(tc.tile_pool(name="hidden", bufs=4))
         results = ctx.enter_context(tc.tile_pool(name="results", bufs=6))
-        psum_relay = ctx.enter_context(tc.psum_pool(name="psum_relay", bufs=2))
-        psum_h = ctx.enter_context(tc.psum_pool(name="psum_h", bufs=3))
+        psum_bias = ctx.enter_context(tc.psum_pool(name="psum_bias", bufs=1))
+        psum_h = ctx.enter_context(tc.psum_pool(name="psum_h", bufs=4))
         psum_o = ctx.enter_context(tc.psum_pool(name="psum_o", bufs=3))
-        ctx.enter_context(tc.manual_schedule())
 
         warm = keep.tile([P, 2], F32)
         nc.vector.memset(warm[:], 0.0)
@@ -61,6 +59,10 @@ def tile_blockmlp_mixerblock_pa_kernel(tc, y0, W1, b1, W2, b2, out):
         b1_rows = NB * H_CHUNKS
         b2_rows = NB * I_CHUNKS
 
+        nc.scalar.dma_start(out=bias_rows[0:b1_rows, :], in_=b1.rearrange("n o (c p) -> (n o c) p", p=P))
+        nc.scalar.dma_start(
+            out=bias_rows[b1_rows : b1_rows + b2_rows, :], in_=b2.rearrange("n o (c p) -> (n o c) p", p=P)
+        )
         y_raw = [keep.tile([P, PACK * BD], BF16, name="y_raw%d" % g) for g in range(G)]
         w1_raw = [keep.tile([P, PACK, H], BF16, name="w1_raw%d" % n) for n in range(NB)]
         w2_raw = [keep.tile([P, H_PASSES, PACK, BD], BF16, name="w2_raw%d" % n) for n in range(NB)]
@@ -78,10 +80,6 @@ def tile_blockmlp_mixerblock_pa_kernel(tc, y0, W1, b1, W2, b2, out):
 
         for g in range(G):
             load_y(g)
-        nc.sync.dma_start(out=bias_rows[0:b1_rows, :], in_=b1.rearrange("n o (c p) -> (n o c) p", p=P))
-        nc.sync.dma_start(
-            out=bias_rows[b1_rows : b1_rows + b2_rows, :], in_=b2.rearrange("n o (c p) -> (n o c) p", p=P)
-        )
         for n in range(NB):
             load_w1(n)
         for n in range(NB):
@@ -93,7 +91,7 @@ def tile_blockmlp_mixerblock_pa_kernel(tc, y0, W1, b1, W2, b2, out):
         b2_col = keep.tile([P, I_CHUNKS, NB], F32)
 
         def biases():
-            bias_t = psum_relay.tile([P, P], BF16, tag="relay")
+            bias_t = psum_bias.tile([P, P], BF16)
             nc.tensor.transpose(bias_t[:], bias_rows[:], ident[:])
             nc.vector.tensor_copy(out=b1_col[:], in_=bias_t[:, 0:b1_rows])
             nc.vector.tensor_copy(
@@ -125,17 +123,6 @@ def tile_blockmlp_mixerblock_pa_kernel(tc, y0, W1, b1, W2, b2, out):
                     z_grouped[g][:, n, :, :].rearrange("p r t -> p (r t)"), z_codes[:, n, b_cols], z_scales[:, n, b_cols]
                 )
 
-        def relay_part(bank_part, planes):
-            nc.tensor.matmul(
-                out=bank_part.rearrange("p c t -> p t c"), lhsT=ident[:], rhs=planes, start=True, stop=True
-            )
-
-        def relay(grouped, planes):
-            bank = psum_relay.tile([P, BANK // K_PASS, P, PACK], BF16, tag="relay")
-            for u in range(BANK // K_PASS):
-                relay_part(bank[:, u, :, :], planes[:, :, u * P : (u + 1) * P])
-            nc.scalar.copy(out=grouped.rearrange("p c t -> p (c t)"), in_=bank[:].rearrange("p u c t -> p (u c t)"))
-
         w1_codes = [keep.tile([P, H], U32, align_bytes=64, name="w1_codes%d" % n) for n in range(NB)]
         w1_scales = [keep.tile([P, H], U8, align_bytes=64, name="w1_scales%d" % n) for n in range(NB)]
         w1_grouped = {}
@@ -145,13 +132,10 @@ def tile_blockmlp_mixerblock_pa_kernel(tc, y0, W1, b1, W2, b2, out):
             regroup(nc.vector.tensor_copy, grouped[:], w1_raw[n][:, :, 0:HALF_H])
             w1_grouped[n, 0] = grouped
 
-        def relay_w1(n, half):
+        def copy_w1_high(n):
             grouped = by_scalar.tile([P, HALF_H, PACK], BF16, align_bytes=64, tag="grouped")
-            width = BANK // PACK
-            for c in range(0, HALF_H, width):
-                j0 = half * HALF_H + c
-                relay(grouped[:, c : c + width, :], w1_raw[n][:, :, j0 : j0 + width])
-            w1_grouped[n, half] = grouped
+            regroup(nc.scalar.copy, grouped[:], w1_raw[n][:, :, HALF_H:H])
+            w1_grouped[n, 1] = grouped
 
         def quantise_w1(n, half):
             j_cols = slice(half * HALF_H, (half + 1) * HALF_H)
@@ -178,18 +162,6 @@ def tile_blockmlp_mixerblock_pa_kernel(tc, y0, W1, b1, W2, b2, out):
 
         def copy_w2_v(c, pair):
             copy_w2(c, pair, by_vector, nc.vector.tensor_copy)
-
-        def relay_w2(c, pair):
-            grouped = by_scalar.tile([P, 2, H_PASSES, P, PACK], BF16, align_bytes=64, tag="grouped")
-            for u in range(2):
-                bank = psum_relay.tile([P, H_PASSES, P, PACK], BF16, tag="relay")
-                for s in range(H_PASSES):
-                    relay_part(bank[:, s, :, :], w2_part(c, 2 * pair + u, s))
-                nc.scalar.copy(
-                    out=grouped[:, u, :, :, :].rearrange("p s c t -> p (s c t)"),
-                    in_=bank[:].rearrange("p s c t -> p (s c t)"),
-                )
-            w2_grouped[c, pair] = grouped
 
         def quantise_w2(c, pair):
             ns = slice(2 * pair, 2 * pair + 2)
@@ -258,80 +230,36 @@ def tile_blockmlp_mixerblock_pa_kernel(tc, y0, W1, b1, W2, b2, out):
                 out=out_rows[g, chunk * P : (chunk + 1) * P, :], in_=o_rows[:].rearrange("p r n -> p (r n)")
             )
 
-        copy_z_v(0)
-        copy_z_s(1)
-        quantise_z(0)
-        copy_z_v(2)
-        copy_z_s(3)
-        quantise_z(1)
-        copy_w1_low(0)
-        relay_w1(0, 1)
-        quantise_z(2)
-        quantise_w1(0, 0)
         biases()
+        copy_z_v(0)
+        quantise_z(0)
+        copy_z_s(1)
+        quantise_z(1)
+        copy_z_v(2)
+        quantise_z(2)
+        copy_z_s(3)
         quantise_z(3)
-        first_layer(0, 0)
+        copy_w1_low(0)
+        copy_w1_high(0)
+        quantise_w1(0, 0)
         quantise_w1(0, 1)
-        copy_w1_low(1)
-        relay_w1(1, 1)
-        first_layer(0, 1)
-        quantise_w1(1, 0)
-        copy_w1_low(2)
-        quantise_w1(1, 1)
-        relay_w1(2, 1)
-        first_layer(1, 0)
-        copy_h(0, 0)
-        quantise_w1(2, 0)
-        quantise_h(0, 0)
-        copy_w1_low(3)
-        first_layer(1, 1)
-        copy_h(0, 1)
-        quantise_w1(2, 1)
-        quantise_h(0, 1)
-        relay_w1(3, 1)
-        first_layer(2, 0)
-        quantise_w1(3, 0)
-        copy_h(1, 0)
-        copy_w2_v(0, 0)
-        quantise_h(1, 0)
-        quantise_w1(3, 1)
-        first_layer(2, 1)
-        copy_h(1, 1)
-        quantise_w2(0, 0)
-        quantise_h(1, 1)
-        copy_w2_v(0, 1)
-        first_layer(3, 0)
-        copy_h(2, 0)
-        quantise_w2(0, 1)
-        quantise_h(2, 0)
-        first_layer(3, 1)
-        relay_w2(1, 0)
-        relay_w2(1, 1)
-        copy_h(2, 1)
-        quantise_h(2, 1)
-        copy_w2_s(2, 0)
-        copy_h(3, 0)
-        quantise_w2(1, 0)
-        copy_w2_s(2, 1)
-        quantise_h(3, 0)
-        copy_h(3, 1)
-        quantise_w2(1, 1)
-        copy_w2_s(3, 0)
-        copy_w2_s(3, 1)
-        quantise_h(3, 1)
-        second_layer(0, 0)
-        second_layer(0, 1)
-        second_layer(0, 2)
-        second_layer(0, 3)
-        quantise_w2(2, 0)
-        for g in range(G):
-            second_layer(1, g)
-        quantise_w2(2, 1)
-        second_layer(2, 0)
-        second_layer(2, 1)
-        quantise_w2(3, 0)
-        second_layer(2, 2)
-        quantise_w2(3, 1)
-        second_layer(2, 3)
-        for g in range(G):
-            second_layer(3, g)
+        for n in range(NB):
+            if n + 1 < NB:
+                copy_w1_low(n + 1)
+                quantise_w1(n + 1, 0)
+                copy_w1_high(n + 1)
+                quantise_w1(n + 1, 1)
+            for s in range(H_PASSES):
+                first_layer(n, s)
+                copy_h(n, s)
+                quantise_h(n, s)
+            if n % 2 == 1:
+                copy_w2_v(0, n // 2)
+                quantise_w2(0, n // 2)
+        for chunk in range(I_CHUNKS):
+            if chunk + 1 < I_CHUNKS:
+                for pair in range(2):
+                    copy_w2_s(chunk + 1, pair)
+                    quantise_w2(chunk + 1, pair)
+            for g in range(G):
+                second_layer(chunk, g)

@@ -59,10 +59,6 @@ def tile_blockmlp_mixerblock_pa_kernel(tc, y0, W1, b1, W2, b2, out):
         b1_rows = NB * H_CHUNKS
         b2_rows = NB * I_CHUNKS
 
-        nc.scalar.dma_start(out=bias_rows[0:b1_rows, :], in_=b1.rearrange("n o (c p) -> (n o c) p", p=P))
-        nc.scalar.dma_start(
-            out=bias_rows[b1_rows : b1_rows + b2_rows, :], in_=b2.rearrange("n o (c p) -> (n o c) p", p=P)
-        )
         y_raw = [keep.tile([P, PACK * BD], BF16, name="y_raw%d" % g) for g in range(G)]
         w1_raw = [keep.tile([P, PACK, H], BF16, name="w1_raw%d" % n) for n in range(NB)]
         w2_raw = [keep.tile([P, H_PASSES, PACK, BD], BF16, name="w2_raw%d" % n) for n in range(NB)]
@@ -78,7 +74,12 @@ def tile_blockmlp_mixerblock_pa_kernel(tc, y0, W1, b1, W2, b2, out):
                 out=w2_raw[n][:], in_=W2[n].rearrange("(s t p) i -> p s t i", s=H_PASSES, t=PACK)
             )
 
-        for g in range(G):
+        load_y(0)
+        nc.sync.dma_start(out=bias_rows[0:b1_rows, :], in_=b1.rearrange("n o (c p) -> (n o c) p", p=P))
+        nc.sync.dma_start(
+            out=bias_rows[b1_rows : b1_rows + b2_rows, :], in_=b2.rearrange("n o (c p) -> (n o c) p", p=P)
+        )
+        for g in range(1, G):
             load_y(g)
         for n in range(NB):
             load_w1(n)
@@ -98,8 +99,8 @@ def tile_blockmlp_mixerblock_pa_kernel(tc, y0, W1, b1, W2, b2, out):
                 out=b2_col[:], in_=bias_t[:, b1_rows : b1_rows + b2_rows].rearrange("p (n c) -> p c n", n=NB)
             )
 
-        z_codes = keep.tile([P, NB, BS], U32, align_bytes=64)
-        z_scales = keep.tile([P, NB, BS], U8, align_bytes=64)
+        z_codes = [keep.tile([P, NB, P], U32, align_bytes=64, name="z_codes%d" % g) for g in range(G)]
+        z_scales = [keep.tile([P, NB, P], U8, align_bytes=64, name="z_scales%d" % g) for g in range(G)]
         z_grouped = {}
 
         def copy_z(g, pool, copy):
@@ -117,11 +118,11 @@ def tile_blockmlp_mixerblock_pa_kernel(tc, y0, W1, b1, W2, b2, out):
             copy_z(g, by_scalar, nc.scalar.copy)
 
         def quantise_z(g):
-            b_cols = slice(g * P, (g + 1) * P)
-            for n in range(NB):
-                quantise(
-                    z_grouped[g][:, n, :, :].rearrange("p r t -> p (r t)"), z_codes[:, n, b_cols], z_scales[:, n, b_cols]
-                )
+            quantise(
+                z_grouped[g][:].rearrange("p n r t -> p (n r t)"),
+                z_codes[g][:].rearrange("p n r -> p (n r)"),
+                z_scales[g][:].rearrange("p n r -> p (n r)"),
+            )
 
         w1_codes = [keep.tile([P, H], U32, align_bytes=64, name="w1_codes%d" % n) for n in range(NB)]
         w1_scales = [keep.tile([P, H], U8, align_bytes=64, name="w1_scales%d" % n) for n in range(NB)]
@@ -176,6 +177,17 @@ def tile_blockmlp_mixerblock_pa_kernel(tc, y0, W1, b1, W2, b2, out):
         h_planes = {}
         h_grouped = {}
 
+        def hidden_pass(acc, n, j_cols, g):
+            nc.tensor.matmul_mx(
+                out=acc,
+                lhsT=w1_codes[n][:, j_cols].bitcast(FP8X4),
+                lhsT_scale=w1_scales[n][:, j_cols],
+                rhs=z_codes[g][:, n, :].bitcast(FP8X4),
+                rhs_scale=z_scales[g][:, n, :],
+                start=True,
+                stop=True,
+            )
+
         def first_layer(n, s):
             planes = hidden.tile([P, PACK, BS], BF16, tag="planes")
             h_planes[n, s] = planes
@@ -183,15 +195,8 @@ def tile_blockmlp_mixerblock_pa_kernel(tc, y0, W1, b1, W2, b2, out):
                 chunk = s * PACK + t
                 j_cols = slice(chunk * P, (chunk + 1) * P)
                 h_acc = psum_h.tile([P, BS], F32)
-                nc.tensor.matmul_mx(
-                    out=h_acc[:],
-                    lhsT=w1_codes[n][:, j_cols].bitcast(FP8X4),
-                    lhsT_scale=w1_scales[n][:, j_cols],
-                    rhs=z_codes[:, n, :].bitcast(FP8X4),
-                    rhs_scale=z_scales[:, n, :],
-                    start=True,
-                    stop=True,
-                )
+                for g in range(G):
+                    hidden_pass(h_acc[:, g * P : (g + 1) * P], n, j_cols, g)
                 bias_at = n * H_CHUNKS + chunk
                 nc.scalar.activation(
                     out=planes[:, t, :], in_=h_acc[:], func=GELU, bias=b1_col[:, bias_at : bias_at + 1], scale=1.0

@@ -45,7 +45,7 @@ def tile_blockmlp_mixerblock_pa_kernel(tc, y0, W1, b1, W2, b2, out):
         by_vector = ctx.enter_context(tc.tile_pool(name="by_vector", bufs=4))
         by_scalar = ctx.enter_context(tc.tile_pool(name="by_scalar", bufs=4))
         hidden = ctx.enter_context(tc.tile_pool(name="hidden", bufs=4))
-        results = ctx.enter_context(tc.tile_pool(name="results", bufs=6))
+        results = ctx.enter_context(tc.tile_pool(name="results", bufs=12))
         psum_bias = ctx.enter_context(tc.psum_pool(name="psum_bias", bufs=1))
         psum_h = ctx.enter_context(tc.psum_pool(name="psum_h", bufs=4))
         psum_o = ctx.enter_context(tc.psum_pool(name="psum_o", bufs=3))
@@ -128,15 +128,15 @@ def tile_blockmlp_mixerblock_pa_kernel(tc, y0, W1, b1, W2, b2, out):
         w1_scales = [keep.tile([P, H], U8, align_bytes=64, name="w1_scales%d" % n) for n in range(NB)]
         w1_grouped = {}
 
-        def copy_w1_low(n):
+        def copy_w1_v(n, half):
             grouped = by_vector.tile([P, HALF_H, PACK], BF16, align_bytes=64, tag="grouped")
-            regroup(nc.vector.tensor_copy, grouped[:], w1_raw[n][:, :, 0:HALF_H])
-            w1_grouped[n, 0] = grouped
+            regroup(nc.vector.tensor_copy, grouped[:], w1_raw[n][:, :, half * HALF_H : (half + 1) * HALF_H])
+            w1_grouped[n, half] = grouped
 
-        def copy_w1_high(n):
+        def copy_w1_s(n, half):
             grouped = by_scalar.tile([P, HALF_H, PACK], BF16, align_bytes=64, tag="grouped")
-            regroup(nc.scalar.copy, grouped[:], w1_raw[n][:, :, HALF_H:H])
-            w1_grouped[n, 1] = grouped
+            regroup(nc.scalar.copy, grouped[:], w1_raw[n][:, :, half * HALF_H : (half + 1) * HALF_H])
+            w1_grouped[n, half] = grouped
 
         def quantise_w1(n, half):
             j_cols = slice(half * HALF_H, (half + 1) * HALF_H)
@@ -160,9 +160,6 @@ def tile_blockmlp_mixerblock_pa_kernel(tc, y0, W1, b1, W2, b2, out):
 
         def copy_w2_s(c, pair):
             copy_w2(c, pair, by_scalar, nc.scalar.copy)
-
-        def copy_w2_v(c, pair):
-            copy_w2(c, pair, by_vector, nc.vector.tensor_copy)
 
         def quantise_w2(c, pair):
             ns = slice(2 * pair, 2 * pair + 2)
@@ -224,16 +221,21 @@ def tile_blockmlp_mixerblock_pa_kernel(tc, y0, W1, b1, W2, b2, out):
                         start=(s == 0),
                         stop=(s == H_PASSES - 1),
                     )
-            o_rows = results.tile([P, P, NB], F32)
-            nc.vector.tensor_tensor(
-                out=o_rows[:],
-                in0=o_acc[:].rearrange("p n r -> p r n"),
-                in1=b2_col[:, chunk, :].unsqueeze(1).to_broadcast([P, P, NB]),
-                op=ADD,
-            )
-            nc.sync.dma_start(
-                out=out_rows[g, chunk * P : (chunk + 1) * P, :], in_=o_rows[:].rearrange("p r n -> p (r n)")
-            )
+            parts = 2 if (chunk, g) == (I_CHUNKS - 1, G - 1) else 1
+            width = P // parts
+            for part in range(parts):
+                r0 = part * width
+                o_rows = results.tile([P, width, NB], F32, tag="o_rows")
+                nc.vector.tensor_tensor(
+                    out=o_rows[:],
+                    in0=o_acc[:, :, r0 : r0 + width].rearrange("p n r -> p r n"),
+                    in1=b2_col[:, chunk, :].unsqueeze(1).to_broadcast([P, width, NB]),
+                    op=ADD,
+                )
+                nc.sync.dma_start(
+                    out=out_rows[g, chunk * P : (chunk + 1) * P, r0 * NB : (r0 + width) * NB],
+                    in_=o_rows[:].rearrange("p r n -> p (r n)"),
+                )
 
         biases()
         copy_z_v(0)
@@ -244,23 +246,23 @@ def tile_blockmlp_mixerblock_pa_kernel(tc, y0, W1, b1, W2, b2, out):
         quantise_z(2)
         copy_z_s(3)
         quantise_z(3)
-        copy_w1_low(0)
-        copy_w1_high(0)
+        copy_w1_v(0, 0)
+        copy_w1_s(0, 1)
         quantise_w1(0, 0)
         quantise_w1(0, 1)
         for n in range(NB):
             if n + 1 < NB:
-                copy_w1_low(n + 1)
+                copy_w1_v(n + 1, 0)
                 quantise_w1(n + 1, 0)
-                copy_w1_high(n + 1)
+                (copy_w1_s if n + 1 < 2 else copy_w1_v)(n + 1, 1)
                 quantise_w1(n + 1, 1)
             for s in range(H_PASSES):
                 first_layer(n, s)
                 copy_h(n, s)
                 quantise_h(n, s)
-            if n % 2 == 1:
-                copy_w2_v(0, n // 2)
-                quantise_w2(0, n // 2)
+        for pair in range(2):
+            copy_w2_s(0, pair)
+            quantise_w2(0, pair)
         for chunk in range(I_CHUNKS):
             if chunk + 1 < I_CHUNKS:
                 for pair in range(2):

from contextlib import ExitStack

import concourse.mybir as mybir
from concourse.masks import make_identity

BF16 = mybir.dt.bfloat16
F32 = mybir.dt.float32
U32 = mybir.dt.uint32
U8 = mybir.dt.uint8
FP8X4 = mybir.dt.float8_e4m3fn_x4
GELU = mybir.ActivationFunctionType.Gelu
ADD = mybir.AluOpType.add

P = 128
PACK = 4
K_PASS = P * PACK

BS, NB, BD, H = 512, 4, 512, 1024
G = BS * NB // BD
H_CHUNKS = H // P
H_PASSES = H // K_PASS
I_CHUNKS = BD // P
HALF_H = H // 2
RUN = 8

FLOPS = 2 * BS * NB * (BD * H + H * BD)


def regroup(copy, grouped, planes):
    copy(
        out=grouped.rearrange("p (c i) t -> p c t i", i=RUN),
        in_=planes.rearrange("p t (c i) -> p c t i", i=RUN),
    )


def tile_blockmlp_mixerblock_pa_kernel(tc, y0, W1, b1, W2, b2, out):
    nc = tc.nc
    out_rows = out.rearrange("a b -> (a b)").rearrange("(g i c) -> g i c", g=G, i=BD)

    def quantise(grouped_flat, codes, scales):
        nc.vector.quantize_mx(out=codes.bitcast(FP8X4), scales=scales, in_=grouped_flat)

    with ExitStack() as ctx:
        keep = ctx.enter_context(tc.tile_pool(name="keep", bufs=1))
        by_vector = ctx.enter_context(tc.tile_pool(name="by_vector", bufs=4))
        by_scalar = ctx.enter_context(tc.tile_pool(name="by_scalar", bufs=4))
        hidden = ctx.enter_context(tc.tile_pool(name="hidden", bufs=4))
        results = ctx.enter_context(tc.tile_pool(name="results", bufs=12))
        psum_bias = ctx.enter_context(tc.psum_pool(name="psum_bias", bufs=1))
        psum_h = ctx.enter_context(tc.psum_pool(name="psum_h", bufs=4))
        psum_o = ctx.enter_context(tc.psum_pool(name="psum_o", bufs=3))

        warm = keep.tile([P, 2], F32)
        nc.vector.memset(warm[:], 0.0)
        nc.scalar.activation(out=warm[:, 1:2], in_=warm[:, 0:1], func=GELU)

        bias_rows = keep.tile([P, P], BF16)
        nc.vector.memset(bias_rows[:], 0.0)
        b1_rows = NB * H_CHUNKS
        b2_rows = NB * I_CHUNKS

        y_raw = [keep.tile([P, PACK * BD], BF16, name="y_raw%d" % g) for g in range(G)]
        w1_raw = [keep.tile([P, PACK, H], BF16, name="w1_raw%d" % n) for n in range(NB)]
        w2_raw = [keep.tile([P, H_PASSES, PACK, BD], BF16, name="w2_raw%d" % n) for n in range(NB)]

        def load_y(g):
            nc.sync.dma_start(out=y_raw[g][:], in_=y0[g * P : (g + 1) * P, :])

        def load_w1(n):
            nc.sync.dma_start(out=w1_raw[n][:], in_=W1[n].rearrange("(p t) j -> p t j", t=PACK))

        def load_w2(n):
            nc.sync.dma_start(
                out=w2_raw[n][:], in_=W2[n].rearrange("(s t p) i -> p s t i", s=H_PASSES, t=PACK)
            )

        load_y(0)
        nc.sync.dma_start(out=bias_rows[0:b1_rows, :], in_=b1.rearrange("n o (c p) -> (n o c) p", p=P))
        nc.sync.dma_start(
            out=bias_rows[b1_rows : b1_rows + b2_rows, :], in_=b2.rearrange("n o (c p) -> (n o c) p", p=P)
        )
        for g in range(1, G):
            load_y(g)
        for n in range(NB):
            load_w1(n)
        for n in range(NB):
            load_w2(n)

        ident = keep.tile([P, P], BF16)
        make_identity(nc, ident[:])
        b1_col = keep.tile([P, b1_rows], F32)
        b2_col = keep.tile([P, I_CHUNKS, NB], F32)

        def biases():
            bias_t = psum_bias.tile([P, P], BF16)
            nc.tensor.transpose(bias_t[:], bias_rows[:], ident[:])
            nc.vector.tensor_copy(out=b1_col[:], in_=bias_t[:, 0:b1_rows])
            nc.vector.tensor_copy(
                out=b2_col[:], in_=bias_t[:, b1_rows : b1_rows + b2_rows].rearrange("p (n c) -> p c n", n=NB)
            )

        z_codes = [keep.tile([P, NB, P], U32, align_bytes=64, name="z_codes%d" % g) for g in range(G)]
        z_scales = [keep.tile([P, NB, P], U8, align_bytes=64, name="z_scales%d" % g) for g in range(G)]
        z_grouped = {}

        def copy_z(g, pool, copy):
            grouped = pool.tile([P, NB, P, PACK], BF16, align_bytes=64, tag="grouped")
            copy(
                out=grouped[:].rearrange("p n r t -> p r t n"),
                in_=y_raw[g][:].rearrange("p (t r n) -> p r t n", t=PACK, n=NB),
            )
            z_grouped[g] = grouped

        def copy_z_v(g):
            copy_z(g, by_vector, nc.vector.tensor_copy)

        def copy_z_s(g):
            copy_z(g, by_scalar, nc.scalar.copy)

        def quantise_z(g):
            quantise(
                z_grouped[g][:].rearrange("p n r t -> p (n r t)"),
                z_codes[g][:].rearrange("p n r -> p (n r)"),
                z_scales[g][:].rearrange("p n r -> p (n r)"),
            )

        w1_codes = [keep.tile([P, H], U32, align_bytes=64, name="w1_codes%d" % n) for n in range(NB)]
        w1_scales = [keep.tile([P, H], U8, align_bytes=64, name="w1_scales%d" % n) for n in range(NB)]
        w1_grouped = {}

        def copy_w1_v(n, half):
            grouped = by_vector.tile([P, HALF_H, PACK], BF16, align_bytes=64, tag="grouped")
            regroup(nc.vector.tensor_copy, grouped[:], w1_raw[n][:, :, half * HALF_H : (half + 1) * HALF_H])
            w1_grouped[n, half] = grouped

        def copy_w1_s(n, half):
            grouped = by_scalar.tile([P, HALF_H, PACK], BF16, align_bytes=64, tag="grouped")
            regroup(nc.scalar.copy, grouped[:], w1_raw[n][:, :, half * HALF_H : (half + 1) * HALF_H])
            w1_grouped[n, half] = grouped

        def quantise_w1(n, half):
            j_cols = slice(half * HALF_H, (half + 1) * HALF_H)
            quantise(
                (w1_grouped[n, half][:].rearrange("p c t -> p (c t)")), w1_codes[n][:, j_cols], w1_scales[n][:, j_cols]
            )

        w2_codes = [keep.tile([P, NB, H_PASSES, P], U32, align_bytes=64, name="w2_codes%d" % c) for c in range(I_CHUNKS)]
        w2_scales = [keep.tile([P, NB, H_PASSES, P], U8, align_bytes=64, name="w2_scales%d" % c) for c in range(I_CHUNKS)]
        w2_grouped = {}

        def w2_part(c, n, s):
            return w2_raw[n][:, s, :, c * P : (c + 1) * P]

        def copy_w2(c, pair, pool, copy):
            grouped = pool.tile([P, 2, H_PASSES, P, PACK], BF16, align_bytes=64, tag="grouped")
            for u in range(2):
                for s in range(H_PASSES):
                    regroup(copy, grouped[:, u, s, :, :], w2_part(c, 2 * pair + u, s))
            w2_grouped[c, pair] = grouped

        def copy_w2_s(c, pair):
            copy_w2(c, pair, by_scalar, nc.scalar.copy)

        def quantise_w2(c, pair):
            ns = slice(2 * pair, 2 * pair + 2)
            quantise(
                w2_grouped[c, pair][:].rearrange("p n s c t -> p (n s c t)"),
                w2_codes[c][:, ns, :, :].rearrange("p n s c -> p (n s c)"),
                w2_scales[c][:, ns, :, :].rearrange("p n s c -> p (n s c)"),
            )

        h_codes = [keep.tile([P, H_PASSES, BS], U32, align_bytes=64, name="h_codes%d" % n) for n in range(NB)]
        h_scales = [keep.tile([P, H_PASSES, BS], U8, align_bytes=64, name="h_scales%d" % n) for n in range(NB)]
        h_planes = {}
        h_grouped = {}

        def hidden_pass(acc, n, j_cols, g):
            nc.tensor.matmul_mx(
                out=acc,
                lhsT=w1_codes[n][:, j_cols].bitcast(FP8X4),
                lhsT_scale=w1_scales[n][:, j_cols],
                rhs=z_codes[g][:, n, :].bitcast(FP8X4),
                rhs_scale=z_scales[g][:, n, :],
                start=True,
                stop=True,
            )

        def first_layer(n, s):
            planes = hidden.tile([P, PACK, BS], BF16, tag="planes")
            h_planes[n, s] = planes
            for t in range(PACK):
                chunk = s * PACK + t
                j_cols = slice(chunk * P, (chunk + 1) * P)
                h_acc = psum_h.tile([P, BS], F32)
                for g in range(G):
                    hidden_pass(h_acc[:, g * P : (g + 1) * P], n, j_cols, g)
                bias_at = n * H_CHUNKS + chunk
                nc.scalar.activation(
                    out=planes[:, t, :], in_=h_acc[:], func=GELU, bias=b1_col[:, bias_at : bias_at + 1], scale=1.0
                )

        def copy_h(n, s):
            grouped = by_vector.tile([P, BS, PACK], BF16, align_bytes=64, tag="grouped")
            regroup(nc.vector.tensor_copy, grouped[:], h_planes[n, s][:])
            h_grouped[n, s] = grouped

        def quantise_h(n, s):
            quantise(h_grouped[n, s][:].rearrange("p c t -> p (c t)"), h_codes[n][:, s, :], h_scales[n][:, s, :])

        def second_layer(chunk, g):
            b_cols = slice(g * P, (g + 1) * P)
            o_acc = psum_o.tile([P, NB, P], F32)
            for n in range(NB):
                for s in range(H_PASSES):
                    nc.tensor.matmul_mx(
                        out=o_acc[:, n, :],
                        lhsT=w2_codes[chunk][:, n, s, :].bitcast(FP8X4),
                        lhsT_scale=w2_scales[chunk][:, n, s, :],
                        rhs=h_codes[n][:, s, b_cols].bitcast(FP8X4),
                        rhs_scale=h_scales[n][:, s, b_cols],
                        start=(s == 0),
                        stop=(s == H_PASSES - 1),
                    )
            parts = 2 if (chunk, g) == (I_CHUNKS - 1, G - 1) else 1
            width = P // parts
            for part in range(parts):
                r0 = part * width
                o_rows = results.tile([P, width, NB], F32, tag="o_rows")
                nc.vector.tensor_tensor(
                    out=o_rows[:],
                    in0=o_acc[:, :, r0 : r0 + width].rearrange("p n r -> p r n"),
                    in1=b2_col[:, chunk, :].unsqueeze(1).to_broadcast([P, width, NB]),
                    op=ADD,
                )
                nc.sync.dma_start(
                    out=out_rows[g, chunk * P : (chunk + 1) * P, r0 * NB : (r0 + width) * NB],
                    in_=o_rows[:].rearrange("p r n -> p (r n)"),
                )

        biases()
        copy_z_v(0)
        quantise_z(0)
        copy_z_s(1)
        quantise_z(1)
        copy_z_v(2)
        quantise_z(2)
        copy_z_s(3)
        quantise_z(3)
        copy_w1_v(0, 0)
        copy_w1_s(0, 1)
        quantise_w1(0, 0)
        quantise_w1(0, 1)
        for n in range(NB):
            if n + 1 < NB:
                copy_w1_v(n + 1, 0)
                quantise_w1(n + 1, 0)
                (copy_w1_s if n + 1 < 2 else copy_w1_v)(n + 1, 1)
                quantise_w1(n + 1, 1)
            for s in range(H_PASSES):
                first_layer(n, s)
                copy_h(n, s)
                quantise_h(n, s)
        for pair in range(2):
            copy_w2_s(0, pair)
            quantise_w2(0, pair)
        for chunk in range(I_CHUNKS):
            if chunk + 1 < I_CHUNKS:
                for pair in range(2):
                    copy_w2_s(chunk + 1, pair)
                    quantise_w2(chunk + 1, pair)
            for g in range(G):
                second_layer(chunk, g)
